import numpy as np
import ml_dtypes


def mxq(x, axis, fmt="e4m3"):
    dtype, down = {"e4m3": (ml_dtypes.float8_e4m3fn, 7), "e5m2": (ml_dtypes.float8_e5m2, 14)}[fmt]
    v = np.moveaxis(np.asarray(x, np.float32).astype(ml_dtypes.bfloat16).astype(np.float64), axis, -1)
    blocks = v.reshape(v.shape[:-1] + (-1, 32))
    amax = np.abs(blocks).max(-1, keepdims=True)
    byte = np.maximum(np.where(amax > 0, np.frexp(amax)[1] - 1 + 127, 0) - down, 1)
    scale = np.exp2(byte - 127.0)
    codes = (blocks / scale).astype(np.float32).astype(dtype).astype(np.float64)
    return np.moveaxis((codes * scale).reshape(v.shape), -1, axis)


WIDE = False


def mx_kscale(k):
    if not WIDE:
        return np.ones(k)
    levels = np.array([10, -10, 5, -5, 0])
    if k % 512:
        return np.exp2(np.random.permutation(np.resize(levels, k // 32))).repeat(32)
    a = np.empty((k // 512, 16))
    for p in range(k // 512):
        a[p, :8] = np.random.permutation(np.resize(levels, 8))
        for g in range(8):
            far = levels[np.abs(levels - a[p, g]) >= 10]
            a[p, g + 8] = far[np.random.randint(len(far))]
    return np.exp2(a.ravel()).repeat(32)


BF16 = ml_dtypes.bfloat16


def bf(x):
    return np.asarray(x, np.float32).astype(BF16)


def f64(x):
    return np.asarray(x).astype(np.float64)


B, S, K, N = 2, 512, 2048, 2048
FP8_MAX = 448.0
EPS = 1e-12


def setup_inputs():
    s = mx_kscale(K)
    return {"x": bf(np.random.standard_normal((B, S, K)) * s),
            "weight": bf(np.random.standard_normal((K, N)) * 1.28 / np.sqrt(K) / s[:, None])}


def reference(x, weight):
    x = f64(x)
    weight = f64(weight)
    b, sl, k = x.shape
    n = weight.shape[1]
    x2 = x.reshape(-1, k)
    x_scale = FP8_MAX / np.maximum(np.max(np.abs(x2)), EPS)
    w_scale = FP8_MAX / np.maximum(np.max(np.abs(weight)), EPS)
    x_sim = np.clip(x2 * x_scale, -FP8_MAX, FP8_MAX)
    w_sim = np.clip(weight * w_scale, -FP8_MAX, FP8_MAX)
    out = (mxq(x_sim, 1, "e4m3") @ mxq(w_sim, 0, "e4m3")) * (1.0 / (x_scale * w_scale))
    return out.reshape(b, sl, n)

@@ -1,0 +1,294 @@
+from contextlib import ExitStack
+
+import concourse.mybir as mybir
+from concourse.masks import make_identity
+
+BF16 = mybir.dt.bfloat16
+F32 = mybir.dt.float32
+I32 = mybir.dt.int32
+U32 = mybir.dt.uint32
+U8 = mybir.dt.uint8
+FP8X4 = mybir.dt.float8_e4m3fn_x4
+ALU = mybir.AluOpType
+ACTF = mybir.ActivationFunctionType
+AX = mybir.AxisListType
+
+P = 128
+M, K, N = 1024, 2048, 2048
+ROW_TILES = M // P
+PACK = 4
+PASSES = K // (P * PACK)
+CHUNK = 512
+CHUNKS = N // CHUNK
+W_LOADS = 2 * PASSES
+UNIT = 2048
+UNITS_PER_SCRATCH = 4
+W_MAXIMA = 2 * W_LOADS // UNITS_PER_SCRATCH
+PAIRS = P
+RUN = 4
+FP8_MAX = 448.0
+EPS = 1e-12
+SIGN_BITS_OFF = 0x7FFF7FFF
+TRANSPOSE_BANKS = 7
+WARM_UP_MATMULS = 4
+
+FLOPS = 2 * M * K * N
+
+
+def tile_modelnew_kernel(tc, x, weight, out):
+    nc = tc.nc
+    x_rows = x.flatten_outer_dims().rearrange("(p i) k -> p i k", i=ROW_TILES)
+    out_rows = out.flatten_outer_dims().rearrange("(p i) n -> p i n", i=ROW_TILES)
+    w_rows = weight.rearrange("(g p u e) n -> p g u (e n)", p=P, u=2, e=2)
+
+    with ExitStack() as ctx:
+        keep = ctx.enter_context(tc.tile_pool(name="keep", bufs=1))
+        slots = ctx.enter_context(tc.tile_pool(name="slots", bufs=ROW_TILES))
+        scratch_pool = ctx.enter_context(tc.tile_pool(name="scratch", bufs=2))
+        out_pool = ctx.enter_context(tc.tile_pool(name="outs", bufs=5))
+        ctx.enter_context(tc.manual_schedule())
+
+        w_sb = keep.tile([P, W_LOADS, 2 * N], BF16)
+        x_sim = keep.tile([P, PASSES, ROW_TILES, PACK * P], BF16, align_bytes=64)
+        x_codes = keep.tile([P, PASSES * ROW_TILES * P], U32, align_bytes=64)
+        x_scale_bytes = keep.tile([P, PASSES * ROW_TILES * P], U8, align_bytes=64)
+        w_codes = keep.tile([P, CHUNKS * PASSES * CHUNK], U32, align_bytes=64)
+        w_scale_bytes = keep.tile([P, CHUNKS * PASSES * CHUNK], U8, align_bytes=64)
+        identity = keep.tile([P, P], F32)
+        identity_over_448 = keep.tile([P, P], F32)
+        x_unit_max = keep.tile([P, ROW_TILES + 1], F32)
+        x_part_max = keep.tile([P, 1], F32)
+        w_part_max = keep.tile([P, W_MAXIMA], F32)
+        x_max_over_448 = keep.tile([P, 1], F32)
+        w_max_over_448 = keep.tile([P, 1], F32)
+        xs = keep.tile([P, 1], F32)
+        ws = keep.tile([P, 1], F32)
+        out_factor = keep.tile([P, 1], F32)
+
+        make_identity(nc, identity[:])
+        nc.vector.memset(x_unit_max[:, ROW_TILES:ROW_TILES + 1], EPS)
+        nc.vector.tensor_scalar(out=identity_over_448[:], in0=identity[:], scalar1=1.0 / FP8_MAX,
+                                scalar2=None, op0=ALU.mult)
+
+        x_sb = []
+        for i in range(ROW_TILES):
+            x_tile = slots.tile([P, K], BF16, name="x_tile%d" % i, tag="slot", align_bytes=64)
+            if i == 0:
+                nc.sync.dma_start(out=x_tile[:, 0:K // 2], in_=x_rows[:, i, 0:K // 2])
+                nc.sync.dma_start(out=x_tile[:, K // 2:K], in_=x_rows[:, i, K // 2:K])
+            else:
+                nc.sync.dma_start(out=x_tile[:], in_=x_rows[:, i, :])
+            x_sb.append(x_tile)
+        for c in range(W_LOADS):
+            nc.sync.dma_start(out=w_sb[:, c, :], in_=w_rows[:, c // 2, c % 2, :])
+
+        scratch_tiles = {}
+
+        def raw_units(u0, u1):
+            if u0 < ROW_TILES:
+                return x_sb[u0][:]
+            c = (u0 - ROW_TILES) // 2
+            lo = ((u0 - ROW_TILES) % 2) * UNIT
+            return w_sb[:, c, lo:lo + (u1 - u0) * UNIT]
+
+        def magnitudes(u0, u1):
+            t = u0 // UNITS_PER_SCRATCH
+            if t not in scratch_tiles:
+                new_scratch = scratch_pool.tile([P, UNITS_PER_SCRATCH * UNIT], BF16, name="magnitudes",
+                                                tag="magnitudes")
+                scratch_tiles[t] = new_scratch
+            first = u0 % UNITS_PER_SCRATCH
+            return scratch_tiles[t][:, first * UNIT:(first + u1 - u0) * UNIT]
+
+        def clear_signs(u0, u1, engine, columns=None):
+            dst = magnitudes(u0, u1)
+            src = raw_units(u0, u1)
+            if columns is not None:
+                dst = dst[:, columns]
+                src = src[:, columns]
+            if engine == "vector":
+                nc.vector.tensor_scalar(out=dst.bitcast(I32), in0=src.bitcast(I32),
+                                        scalar1=SIGN_BITS_OFF, scalar2=None, op0=ALU.bitwise_and)
+            else:
+                nc.scalar.activation(out=dst, in_=src, func=ACTF.Abs)
+
+        def max_of_w_units(u0, u1):
+            mags = magnitudes(u0, u1)
+            n = (u0 - ROW_TILES) // UNITS_PER_SCRATCH
+            first_value = EPS if n == 0 else w_part_max[:, n - 1:n]
+            nc.vector.tensor_scalar(out=mags, in0=mags, scalar1=1.0, scalar2=first_value,
+                                    op0=ALU.mult, op1=ALU.max, accum_out=w_part_max[:, n:n + 1])
+
+        def max_of_x_unit(i):
+            mags = magnitudes(i, i + 1)
+            nc.vector.tensor_scalar(out=mags, in0=mags, scalar1=1.0, scalar2=None,
+                                    op0=ALU.mult, op1=ALU.max, accum_out=x_unit_max[:, i:i + 1])
+
+        def quantise_x(g, i0, i1):
+            a0, a1 = (g * ROW_TILES + i0) * P, (g * ROW_TILES + i1) * P
+            nc.vector.quantize_mx(out=x_codes[:, a0:a1].bitcast(FP8X4), scales=x_scale_bytes[:, a0:a1],
+                                  in_=x_sim[:, g, i0:i1, :].rearrange("p i c -> p (i c)"))
+
+        with tc.psum_pool(name="psum1", bufs=TRANSPOSE_BANKS) as psum1:
+            transposed = {}
+
+            def transpose_x(n):
+                h, i = n // ROW_TILES, n % ROW_TILES
+                pairs = x_sb[i][:].bitcast(F32)
+                bank = psum1.tile([P, 2, 2, P], F32, name="bank", tag="bank")
+                for gg in range(2):
+                    for u in range(2):
+                        g0 = 2 * PAIRS * (2 * h + gg)
+                        nc.tensor.transpose(bank[:, u, gg, :], pairs[:, g0 + u:g0 + 2 * PAIRS:2], identity[:])
+                transposed[n] = bank
+
+            def scale_x(n):
+                h, i = n // ROW_TILES, n % ROW_TILES
+                nc.scalar.activation(
+                    out=x_sim[:, 2 * h:2 * h + 2, i, :].rearrange("p g (r u e) -> p g r u e", u=2, e=2),
+                    in_=transposed[n][:].bitcast(BF16).rearrange("p u g (r e) -> p g r u e", e=2),
+                    func=ACTF.Copy, scale=xs[:, 0:1])
+                if n + TRANSPOSE_BANKS < 2 * ROW_TILES:
+                    transpose_x(n + TRANSPOSE_BANKS)
+
+            def spread(column, name):
+                everywhere = psum1.tile([P, P], F32, name=name, tag="spread", bufs=1)
+                nc.tensor.matmul(out=everywhere[:], lhsT=column.to_broadcast([P, P]),
+                                 rhs=identity_over_448[:], start=True, stop=True)
+                return everywhere
+
+            def scale_from(everywhere, max_over_448, scale):
+                nc.vector.tensor_reduce(out=max_over_448[:], in_=everywhere[:], axis=AX.X, op=ALU.max)
+                nc.vector.reciprocal(out=scale[:], in_=max_over_448[:])
+
+            for n in range(TRANSPOSE_BANKS):
+                transpose_x(n)
+
+            clear_signs(0, 1, "vector", slice(0, K // 2))
+            clear_signs(0, 1, "vector", slice(K // 2, K))
+            max_of_x_unit(0)
+            clear_signs(1, 2, "vector")
+            max_of_x_unit(1)
+            clear_signs(2, 3, "scalar")
+            clear_signs(3, 4, "vector")
+            max_of_x_unit(3)
+            clear_signs(4, 5, "scalar")
+            clear_signs(5, 6, "vector")
+            max_of_x_unit(2)
+            max_of_x_unit(5)
+            clear_signs(6, 7, "scalar")
+            clear_signs(7, 8, "vector")
+            max_of_x_unit(4)
+            max_of_x_unit(7)
+            clear_signs(8, 10, "scalar")
+            max_of_x_unit(6)
+            nc.vector.tensor_reduce(out=x_part_max[:], in_=x_unit_max[:], axis=AX.X, op=ALU.max)
+            x_everywhere = spread(x_part_max[:, 0:1], "x_everywhere")
+            clear_signs(10, 12, "vector")
+            scale_from(x_everywhere, x_max_over_448, xs)
+            for n in range(ROW_TILES):
+                scale_x(n)
+            clear_signs(12, 14, "vector")
+            max_of_w_units(8, 12)
+            clear_signs(14, 16, "vector")
+            clear_signs(16, 18, "vector")
+            clear_signs(18, 20, "scalar")
+            for n in range(ROW_TILES, 2 * ROW_TILES):
+                scale_x(n)
+            max_of_w_units(12, 16)
+            clear_signs(20, 22, "vector")
+            clear_signs(22, 24, "vector")
+            max_of_w_units(16, 20)
+            max_of_w_units(20, 24)
+            w_everywhere = spread(w_part_max[:, W_MAXIMA - 1:W_MAXIMA], "w_everywhere")
+            warm_up = psum1.tile([P, CHUNK], F32, name="warm_up", tag="bank")
+            for d in range(WARM_UP_MATMULS):
+                nc.tensor.matmul(out=warm_up[:], lhsT=w_sb[:, 0, 0:P], rhs=w_sb[:, 0, 0:CHUNK],
+                                 start=True, stop=True)
+            quantise_x(0, 0, ROW_TILES // 2)
+            scale_from(w_everywhere, w_max_over_448, ws)
+
+        w_by_row = w_sb[:].rearrange("p c (e n) -> p (c e) n", e=2)
+        panels = {}
+
+        def scale_w(j, g, engine):
+            panel = slots.tile([P, PACK * CHUNK], BF16, name="panel", tag="slot", align_bytes=64)
+            src = w_by_row[:, PACK * g:PACK * g + PACK, j * CHUNK:(j + 1) * CHUNK].rearrange(
+                "p t (c i) -> p c t i", i=RUN)
+            dst = panel[:].rearrange("p (c i t) -> p c t i", i=RUN, t=PACK)
+            if engine == "vector":
+                nc.vector.tensor_scalar(out=dst, in0=src, scalar1=ws[:, 0:1], scalar2=None,
+                                        op0=ALU.mult)
+            else:
+                nc.scalar.activation(out=dst, in_=src, func=ACTF.Copy, scale=ws[:, 0:1])
+            panels[(j, g)] = panel
+
+        def quantise_w(j, g):
+            b = (j * PASSES + g) * CHUNK
+            nc.vector.quantize_mx(out=w_codes[:, b:b + CHUNK].bitcast(FP8X4), scales=w_scale_bytes[:, b:b + CHUNK],
+                                  in_=panels[(j, g)][:])
+
+        def mx_pass(acc, i, j, g, c0=0, c1=CHUNK):
+            a = (g * ROW_TILES + i) * P
+            b = (j * PASSES + g) * CHUNK
+            nc.tensor.matmul_mx(out=acc[:], lhsT=x_codes[:, a:a + P].bitcast(FP8X4),
+                                lhsT_scale=x_scale_bytes[:, a:a + P],
+                                rhs=w_codes[:, b + c0:b + c1].bitcast(FP8X4),
+                                rhs_scale=w_scale_bytes[:, b + c0:b + c1],
+                                start=(g == 0), stop=(g == PASSES - 1))
+
+        def finish(acc, i, j, engine, c0=0, c1=CHUNK):
+            result = out_pool.tile([P, CHUNK], F32, name="result", tag="result")
+            if engine == "vector":
+                nc.vector.tensor_scalar(out=result[:, c0:c1], in0=acc[:], scalar1=out_factor[:, 0:1],
+                                        scalar2=None, op0=ALU.mult)
+            else:
+                nc.scalar.activation(out=result[:, c0:c1], in_=acc[:], func=ACTF.Copy,
+                                     scale=out_factor[:, 0:1])
+            nc.sync.dma_start(out=out_rows[:, i, j * CHUNK + c0:j * CHUNK + c1], in_=result[:, c0:c1])
+
+        with tc.psum_pool(name="psum2", bufs=ROW_TILES) as psum2:
+            scale_w(0, 0, "vector")
+            quantise_w(0, 0)
+            scale_w(0, 1, "scalar")
+            scale_w(0, 2, "scalar")
+            scale_w(0, 3, "scalar")
+            quantise_x(0, ROW_TILES // 2, ROW_TILES)
+            for g in range(1, PASSES):
+                quantise_x(g, 0, ROW_TILES)
+                quantise_w(0, g)
+            accs = {}
+            for i in range(ROW_TILES):
+                first_acc = psum2.tile([P, CHUNK], F32, name="acc", tag="acc")
+                accs[i] = first_acc
+            for g in range(PASSES):
+                for i in range(ROW_TILES):
+                    mx_pass(accs[i], i, 0, g)
+            nc.vector.tensor_tensor(out=out_factor[:], in0=x_max_over_448[:], in1=w_max_over_448[:],
+                                    op=ALU.mult)
+            for j in range(1, CHUNKS):
+                first_on_scalar = 2 if j == 1 else 3
+                for g in range(first_on_scalar, PASSES):
+                    scale_w(j, g, "scalar")
+                for g in range(first_on_scalar):
+                    scale_w(j, g, "vector")
+                    if g > 0:
+                        quantise_w(j, g - 1)
+                for g in range(first_on_scalar - 1, PASSES):
+                    quantise_w(j, g)
+                for i in range(ROW_TILES):
+                    finish(accs[i], i, j - 1, "scalar")
+                for i in range(ROW_TILES if j < CHUNKS - 1 else ROW_TILES - 1):
+                    acc = psum2.tile([P, CHUNK], F32, name="acc", tag="acc")
+                    accs[i] = acc
+                    for g in range(PASSES):
+                        mx_pass(acc, i, j, g)
+            for i in range(ROW_TILES - 1):
+                finish(accs[i], i, CHUNKS - 1, "vector" if i % 2 else "scalar")
+            for half in range(2):
+                c0 = half * (CHUNK // 2)
+                half_acc = psum2.tile([P, CHUNK // 2], F32, name="half_acc", tag="acc")
+                for g in range(PASSES):
+                    mx_pass(half_acc, ROW_TILES - 1, CHUNKS - 1, g, c0, c0 + CHUNK // 2)
+                finish(half_acc, ROW_TILES - 1, CHUNKS - 1, "vector" if half == 0 else "scalar",
+                       c0, c0 + CHUNK // 2)

@@ -23,8 +23,11 @@ CHUNKS = N // CHUNK
 W_LOADS = 2 * PASSES
 UNIT = 2048
 UNITS_PER_SCRATCH = 4
-W_MAXIMA = 2 * W_LOADS // UNITS_PER_SCRATCH
+X_MAXIMA = 5
+W_MAXIMA = 4
 PAIRS = P
+VECTOR_SHARE = 352
+FIRST_ON_SCALAR = 3
 RUN = 4
 FP8_MAX = 448.0
 EPS = 1e-12
@@ -44,8 +47,6 @@ def tile_modelnew_kernel(tc, x, weight, out):
     with ExitStack() as ctx:
         keep = ctx.enter_context(tc.tile_pool(name="keep", bufs=1))
         slots = ctx.enter_context(tc.tile_pool(name="slots", bufs=ROW_TILES))
-        scratch_pool = ctx.enter_context(tc.tile_pool(name="scratch", bufs=2))
-        out_pool = ctx.enter_context(tc.tile_pool(name="outs", bufs=5))
         ctx.enter_context(tc.manual_schedule())
 
         w_sb = keep.tile([P, W_LOADS, 2 * N], BF16)
@@ -55,8 +56,9 @@ def tile_modelnew_kernel(tc, x, weight, out):
         w_codes = keep.tile([P, CHUNKS * PASSES * CHUNK], U32, align_bytes=64)
         w_scale_bytes = keep.tile([P, CHUNKS * PASSES * CHUNK], U8, align_bytes=64)
         identity = keep.tile([P, P], F32)
-        identity_over_448 = keep.tile([P, P], F32)
-        x_unit_max = keep.tile([P, ROW_TILES + 1], F32)
+        identity_bf16 = keep.tile([P, P], BF16)
+        spread_out = keep.tile([P, P], F32)
+        x_unit_max = keep.tile([P, X_MAXIMA], F32)
         x_part_max = keep.tile([P, 1], F32)
         w_part_max = keep.tile([P, W_MAXIMA], F32)
         x_max_over_448 = keep.tile([P, 1], F32)
@@ -66,9 +68,7 @@ def tile_modelnew_kernel(tc, x, weight, out):
         out_factor = keep.tile([P, 1], F32)
 
         make_identity(nc, identity[:])
-        nc.vector.memset(x_unit_max[:, ROW_TILES:ROW_TILES + 1], EPS)
-        nc.vector.tensor_scalar(out=identity_over_448[:], in0=identity[:], scalar1=1.0 / FP8_MAX,
-                                scalar2=None, op0=ALU.mult)
+        nc.vector.tensor_copy(out=identity_bf16[:], in_=identity[:])
 
         x_sb = []
         for i in range(ROW_TILES):
@@ -87,9 +87,7 @@ def tile_modelnew_kernel(tc, x, weight, out):
         def raw_units(u0, u1):
             if u0 < ROW_TILES:
                 return x_sb[u0][:]
-            c = (u0 - ROW_TILES) // 2
-            lo = ((u0 - ROW_TILES) % 2) * UNIT
-            return w_sb[:, c, lo:lo + (u1 - u0) * UNIT]
+            return w_sb[:].rearrange("p c n -> p (c n)")[:, (u0 - ROW_TILES) * UNIT:(u1 - ROW_TILES) * UNIT]
 
         def magnitudes(u0, u1):
             t = u0 // UNITS_PER_SCRATCH
@@ -112,15 +110,22 @@ def tile_modelnew_kernel(tc, x, weight, out):
             else:
                 nc.scalar.activation(out=dst, in_=src, func=ACTF.Abs)
 
+        w_steps = []
+
         def max_of_w_units(u0, u1):
             mags = magnitudes(u0, u1)
-            n = (u0 - ROW_TILES) // UNITS_PER_SCRATCH
-            first_value = EPS if n == 0 else w_part_max[:, n - 1:n]
+            n = len(w_steps)
+            w_steps.append(u0)
+            first_value = 0.0 if n == 0 else w_part_max[:, n - 1:n]
             nc.vector.tensor_scalar(out=mags, in0=mags, scalar1=1.0, scalar2=first_value,
                                     op0=ALU.mult, op1=ALU.max, accum_out=w_part_max[:, n:n + 1])
 
-        def max_of_x_unit(i):
-            mags = magnitudes(i, i + 1)
+        x_steps = []
+
+        def max_of_x_units(u0, u1):
+            mags = magnitudes(u0, u1)
+            i = len(x_steps)
+            x_steps.append(u0)
             nc.vector.tensor_scalar(out=mags, in0=mags, scalar1=1.0, scalar2=None,
                                     op0=ALU.mult, op1=ALU.max, accum_out=x_unit_max[:, i:i + 1])
 
@@ -129,76 +134,89 @@ def tile_modelnew_kernel(tc, x, weight, out):
             nc.vector.quantize_mx(out=x_codes[:, a0:a1].bitcast(FP8X4), scales=x_scale_bytes[:, a0:a1],
                                   in_=x_sim[:, g, i0:i1, :].rearrange("p i c -> p (i c)"))
 
-        with tc.psum_pool(name="psum1", bufs=TRANSPOSE_BANKS) as psum1:
+        with tc.psum_pool(name="psum1", bufs=TRANSPOSE_BANKS) as psum1, tc.tile_pool(name="scratch", bufs=3) as scratch_pool:
             transposed = {}
 
-            def transpose_x(n):
-                h, i = n // ROW_TILES, n % ROW_TILES
+            def transpose_x(h, i):
                 pairs = x_sb[i][:].bitcast(F32)
                 bank = psum1.tile([P, 2, 2, P], F32, name="bank", tag="bank")
                 for gg in range(2):
                     for u in range(2):
                         g0 = 2 * PAIRS * (2 * h + gg)
                         nc.tensor.transpose(bank[:, u, gg, :], pairs[:, g0 + u:g0 + 2 * PAIRS:2], identity[:])
-                transposed[n] = bank
+                transposed[(h, i)] = bank
 
-            def scale_x(n):
-                h, i = n // ROW_TILES, n % ROW_TILES
-                nc.scalar.activation(
-                    out=x_sim[:, 2 * h:2 * h + 2, i, :].rearrange("p g (r u e) -> p g r u e", u=2, e=2),
-                    in_=transposed[n][:].bitcast(BF16).rearrange("p u g (r e) -> p g r u e", e=2),
-                    func=ACTF.Copy, scale=xs[:, 0:1])
-                if n + TRANSPOSE_BANKS < 2 * ROW_TILES:
-                    transpose_x(n + TRANSPOSE_BANKS)
+            def copy_raw_x(h, i):
+                nc.scalar.copy(
+                    out=x_sim[:, 2 * h:2 * h + 2, i, :].bitcast(F32).rearrange("p g (r u) -> p g r u", u=2),
+                    in_=transposed[(h, i)][:].rearrange("p u g r -> p g r u"))
+
+            def scale_x(g, i0, i1):
+                part = x_sim[:, g, i0:i1, :].rearrange("p i c -> p (i c)")
+                nc.gpsimd.tensor_scalar(out=part, in0=part, scalar1=xs[:, 0:1], scalar2=1.0,
+                                        op0=ALU.mult, op1=ALU.mult)
 
             def spread(column, name):
                 everywhere = psum1.tile([P, P], F32, name=name, tag="spread", bufs=1)
-                nc.tensor.matmul(out=everywhere[:], lhsT=column.to_broadcast([P, P]),
-                                 rhs=identity_over_448[:], start=True, stop=True)
+                nc.tensor.matmul(out=everywhere[:], lhsT=column.bitcast(BF16)[:, 1:2].to_broadcast([P, P]),
+                                 rhs=identity_bf16[:], start=True, stop=True)
                 return everywhere
 
             def scale_from(everywhere, max_over_448, scale):
-                nc.vector.tensor_reduce(out=max_over_448[:], in_=everywhere[:], axis=AX.X, op=ALU.max)
+                nc.vector.tensor_scalar(out=spread_out[:], in0=everywhere[:], scalar1=1.0 / FP8_MAX, scalar2=EPS / FP8_MAX,
+                                        op0=ALU.mult, op1=ALU.max, accum_out=max_over_448[:])
                 nc.vector.reciprocal(out=scale[:], in_=max_over_448[:])
 
-            for n in range(TRANSPOSE_BANKS):
-                transpose_x(n)
-
+            for i in range(TRANSPOSE_BANKS):
+                transpose_x(0, i)
             clear_signs(0, 1, "vector", slice(0, K // 2))
             clear_signs(0, 1, "vector", slice(K // 2, K))
-            max_of_x_unit(0)
+            max_of_x_units(0, 1)
             clear_signs(1, 2, "vector")
-            max_of_x_unit(1)
+            max_of_x_units(1, 2)
+            copy_raw_x(0, 0)
+            transpose_x(0, 7)
             clear_signs(2, 3, "scalar")
             clear_signs(3, 4, "vector")
-            max_of_x_unit(3)
+            max_of_x_units(2, 4)
             clear_signs(4, 5, "scalar")
             clear_signs(5, 6, "vector")
-            max_of_x_unit(2)
-            max_of_x_unit(5)
+            for i in range(1, 4):
+                copy_raw_x(0, i)
+                transpose_x(1, i - 1)
             clear_signs(6, 7, "scalar")
+            max_of_x_units(4, 6)
             clear_signs(7, 8, "vector")
-            max_of_x_unit(4)
-            max_of_x_unit(7)
-            clear_signs(8, 10, "scalar")
-            max_of_x_unit(6)
+            clear_signs(8, 10, "vector")
+            for i in range(4, ROW_TILES):
+                copy_raw_x(0, i)
+                transpose_x(1, i - 1)
+            max_of_x_units(6, 8)
             nc.vector.tensor_reduce(out=x_part_max[:], in_=x_unit_max[:], axis=AX.X, op=ALU.max)
             x_everywhere = spread(x_part_max[:, 0:1], "x_everywhere")
             clear_signs(10, 12, "vector")
             scale_from(x_everywhere, x_max_over_448, xs)
-            for n in range(ROW_TILES):
-                scale_x(n)
-            clear_signs(12, 14, "vector")
+            for g in range(2):
+                for i in range(0, ROW_TILES, 2):
+                    scale_x(g, i, i + 2)
+            copy_raw_x(1, 0)
+            transpose_x(1, 7)
+            clear_signs(12, 14, "scalar")
             max_of_w_units(8, 12)
+            clear_signs(16, 18, "scalar")
             clear_signs(14, 16, "vector")
-            clear_signs(16, 18, "vector")
-            clear_signs(18, 20, "scalar")
-            for n in range(ROW_TILES, 2 * ROW_TILES):
-                scale_x(n)
             max_of_w_units(12, 16)
-            clear_signs(20, 22, "vector")
-            clear_signs(22, 24, "vector")
+            for i in range(1, 5):
+                copy_raw_x(1, i)
+            clear_signs(20, 23, "scalar")
+            clear_signs(18, 20, "vector")
             max_of_w_units(16, 20)
+            for i in range(5, ROW_TILES):
+                copy_raw_x(1, i)
+            for g in range(2, PASSES):
+                for i in range(0, ROW_TILES, 2):
+                    scale_x(g, i, i + 2)
+            clear_signs(23, 24, "vector")
             max_of_w_units(20, 24)
             w_everywhere = spread(w_part_max[:, W_MAXIMA - 1:W_MAXIMA], "w_everywhere")
             warm_up = psum1.tile([P, CHUNK], F32, name="warm_up", tag="bank")
@@ -211,17 +229,19 @@ def tile_modelnew_kernel(tc, x, weight, out):
         w_by_row = w_sb[:].rearrange("p c (e n) -> p (c e) n", e=2)
         panels = {}
 
-        def scale_w(j, g, engine):
-            panel = slots.tile([P, PACK * CHUNK], BF16, name="panel", tag="slot", align_bytes=64)
-            src = w_by_row[:, PACK * g:PACK * g + PACK, j * CHUNK:(j + 1) * CHUNK].rearrange(
+        def scale_w(j, g, engine, c0=0, c1=CHUNK):
+            if c0 == 0:
+                new_panel = slots.tile([P, PACK * CHUNK], BF16, name="panel", tag="slot", align_bytes=64)
+                panels[(j, g)] = new_panel
+            panel = panels[(j, g)]
+            src = w_by_row[:, PACK * g:PACK * g + PACK, j * CHUNK + c0:j * CHUNK + c1].rearrange(
                 "p t (c i) -> p c t i", i=RUN)
-            dst = panel[:].rearrange("p (c i t) -> p c t i", i=RUN, t=PACK)
+            dst = panel[:, PACK * c0:PACK * c1].rearrange("p (c i t) -> p c t i", i=RUN, t=PACK)
             if engine == "vector":
                 nc.vector.tensor_scalar(out=dst, in0=src, scalar1=ws[:, 0:1], scalar2=None,
                                         op0=ALU.mult)
             else:
                 nc.scalar.activation(out=dst, in_=src, func=ACTF.Copy, scale=ws[:, 0:1])
-            panels[(j, g)] = panel
 
         def quantise_w(j, g):
             b = (j * PASSES + g) * CHUNK
@@ -247,13 +267,14 @@ def tile_modelnew_kernel(tc, x, weight, out):
                                      scale=out_factor[:, 0:1])
             nc.sync.dma_start(out=out_rows[:, i, j * CHUNK + c0:j * CHUNK + c1], in_=result[:, c0:c1])
 
-        with tc.psum_pool(name="psum2", bufs=ROW_TILES) as psum2:
-            scale_w(0, 0, "vector")
+        with tc.psum_pool(name="psum2", bufs=ROW_TILES) as psum2, tc.tile_pool(name="outs", bufs=5) as out_pool:
+            scale_w(0, 0, "vector", 0, VECTOR_SHARE)
+            scale_w(0, 0, "scalar", VECTOR_SHARE, CHUNK)
             quantise_w(0, 0)
+            quantise_x(0, ROW_TILES // 2, ROW_TILES)
             scale_w(0, 1, "scalar")
             scale_w(0, 2, "scalar")
             scale_w(0, 3, "scalar")
-            quantise_x(0, ROW_TILES // 2, ROW_TILES)
             for g in range(1, PASSES):
                 quantise_x(g, 0, ROW_TILES)
                 quantise_w(0, g)
@@ -267,22 +288,24 @@ def tile_modelnew_kernel(tc, x, weight, out):
             nc.vector.tensor_tensor(out=out_factor[:], in0=x_max_over_448[:], in1=w_max_over_448[:],
                                     op=ALU.mult)
             for j in range(1, CHUNKS):
-                first_on_scalar = 2 if j == 1 else 3
-                for g in range(first_on_scalar, PASSES):
+                for g in range(FIRST_ON_SCALAR, PASSES):
                     scale_w(j, g, "scalar")
-                for g in range(first_on_scalar):
+                for g in range(FIRST_ON_SCALAR):
                     scale_w(j, g, "vector")
                     if g > 0:
                         quantise_w(j, g - 1)
-                for g in range(first_on_scalar - 1, PASSES):
+                for g in range(FIRST_ON_SCALAR - 1, PASSES):
                     quantise_w(j, g)
                 for i in range(ROW_TILES):
                     finish(accs[i], i, j - 1, "scalar")
-                for i in range(ROW_TILES if j < CHUNKS - 1 else ROW_TILES - 1):
-                    acc = psum2.tile([P, CHUNK], F32, name="acc", tag="acc")
-                    accs[i] = acc
+                in_step = ROW_TILES // 2 if j == 1 else 1
+                for i0 in range(0, ROW_TILES if j < CHUNKS - 1 else ROW_TILES - 1, in_step):
+                    for i in range(i0, i0 + in_step):
+                        acc = psum2.tile([P, CHUNK], F32, name="acc", tag="acc")
+                        accs[i] = acc
                     for g in range(PASSES):
-                        mx_pass(acc, i, j, g)
+                        for i in range(i0, i0 + in_step):
+                            mx_pass(accs[i], i, j, g)
             for i in range(ROW_TILES - 1):
                 finish(accs[i], i, CHUNKS - 1, "vector" if i % 2 else "scalar")
             for half in range(2):

@@ -146,15 +146,11 @@ def tile_modelnew_kernel(tc, x, weight, out):
                         nc.tensor.transpose(bank[:, u, gg, :], pairs[:, g0 + u:g0 + 2 * PAIRS:2], identity[:])
                 transposed[(h, i)] = bank
 
-            def copy_raw_x(h, i):
-                nc.scalar.copy(
-                    out=x_sim[:, 2 * h:2 * h + 2, i, :].bitcast(F32).rearrange("p g (r u) -> p g r u", u=2),
-                    in_=transposed[(h, i)][:].rearrange("p u g r -> p g r u"))
-
-            def scale_x(g, i0, i1):
-                part = x_sim[:, g, i0:i1, :].rearrange("p i c -> p (i c)")
-                nc.gpsimd.tensor_scalar(out=part, in0=part, scalar1=xs[:, 0:1], scalar2=1.0,
-                                        op0=ALU.mult, op1=ALU.mult)
+            def scale_x(h, i):
+                nc.scalar.activation(
+                    out=x_sim[:, 2 * h:2 * h + 2, i, :].rearrange("p g (r u e) -> p g r u e", u=2, e=2),
+                    in_=transposed[(h, i)][:].bitcast(BF16).rearrange("p u g (r e) -> p g r u e", e=2),
+                    func=ACTF.Copy, scale=xs[:, 0:1])
 
             def spread(column, name):
                 everywhere = psum1.tile([P, P], F32, name=name, tag="spread", bufs=1)
@@ -174,49 +170,40 @@ def tile_modelnew_kernel(tc, x, weight, out):
             max_of_x_units(0, 1)
             clear_signs(1, 2, "vector")
             max_of_x_units(1, 2)
-            copy_raw_x(0, 0)
-            transpose_x(0, 7)
             clear_signs(2, 3, "scalar")
             clear_signs(3, 4, "vector")
             max_of_x_units(2, 4)
             clear_signs(4, 5, "scalar")
             clear_signs(5, 6, "vector")
-            for i in range(1, 4):
-                copy_raw_x(0, i)
-                transpose_x(1, i - 1)
             clear_signs(6, 7, "scalar")
             max_of_x_units(4, 6)
             clear_signs(7, 8, "vector")
-            clear_signs(8, 10, "vector")
-            for i in range(4, ROW_TILES):
-                copy_raw_x(0, i)
-                transpose_x(1, i - 1)
+            clear_signs(8, 10, "scalar")
             max_of_x_units(6, 8)
             nc.vector.tensor_reduce(out=x_part_max[:], in_=x_unit_max[:], axis=AX.X, op=ALU.max)
             x_everywhere = spread(x_part_max[:, 0:1], "x_everywhere")
             clear_signs(10, 12, "vector")
             scale_from(x_everywhere, x_max_over_448, xs)
-            for g in range(2):
-                for i in range(0, ROW_TILES, 2):
-                    scale_x(g, i, i + 2)
-            copy_raw_x(1, 0)
-            transpose_x(1, 7)
-            clear_signs(12, 14, "scalar")
             max_of_w_units(8, 12)
-            clear_signs(16, 18, "scalar")
-            clear_signs(14, 16, "vector")
+            for i in range(2):
+                scale_x(0, i)
+            transpose_x(0, 7)
+            transpose_x(1, 0)
+            clear_signs(14, 16, "scalar")
+            clear_signs(12, 14, "vector")
+            clear_signs(16, 18, "vector")
             max_of_w_units(12, 16)
-            for i in range(1, 5):
-                copy_raw_x(1, i)
-            clear_signs(20, 23, "scalar")
+            for i in range(2, ROW_TILES):
+                scale_x(0, i)
+                transpose_x(1, i - 1)
             clear_signs(18, 20, "vector")
+            clear_signs(20, 22, "vector")
             max_of_w_units(16, 20)
-            for i in range(5, ROW_TILES):
-                copy_raw_x(1, i)
-            for g in range(2, PASSES):
-                for i in range(0, ROW_TILES, 2):
-                    scale_x(g, i, i + 2)
-            clear_signs(23, 24, "vector")
+            for i in range(ROW_TILES):
+                scale_x(1, i)
+                if i == 0:
+                    transpose_x(1, 7)
+            clear_signs(22, 24, "vector")
             max_of_w_units(20, 24)
             w_everywhere = spread(w_part_max[:, W_MAXIMA - 1:W_MAXIMA], "w_everywhere")
             warm_up = psum1.tile([P, CHUNK], F32, name="warm_up", tag="bank")

@@ -23,7 +23,7 @@ CHUNKS = N // CHUNK
 W_LOADS = 2 * PASSES
 UNIT = 2048
 UNITS_PER_SCRATCH = 4
-X_MAXIMA = 5
+X_MAXIMA = 8
 W_MAXIMA = 4
 PAIRS = P
 VECTOR_SHARE = 352
@@ -172,25 +172,28 @@ def tile_modelnew_kernel(tc, x, weight, out):
             max_of_x_units(1, 2)
             clear_signs(2, 3, "scalar")
             clear_signs(3, 4, "vector")
-            max_of_x_units(2, 4)
+            max_of_x_units(3, 4)
             clear_signs(4, 5, "scalar")
             clear_signs(5, 6, "vector")
+            max_of_x_units(2, 3)
+            max_of_x_units(5, 6)
             clear_signs(6, 7, "scalar")
-            max_of_x_units(4, 6)
             clear_signs(7, 8, "vector")
+            max_of_x_units(4, 5)
+            max_of_x_units(7, 8)
             clear_signs(8, 10, "scalar")
-            max_of_x_units(6, 8)
+            max_of_x_units(6, 7)
             nc.vector.tensor_reduce(out=x_part_max[:], in_=x_unit_max[:], axis=AX.X, op=ALU.max)
             x_everywhere = spread(x_part_max[:, 0:1], "x_everywhere")
             clear_signs(10, 12, "vector")
             scale_from(x_everywhere, x_max_over_448, xs)
+            clear_signs(12, 14, "vector")
             max_of_w_units(8, 12)
             for i in range(2):
                 scale_x(0, i)
             transpose_x(0, 7)
             transpose_x(1, 0)
             clear_signs(14, 16, "scalar")
-            clear_signs(12, 14, "vector")
             clear_signs(16, 18, "vector")
             max_of_w_units(12, 16)
             for i in range(2, ROW_TILES):

@@ -178,7 +178,8 @@ def tile_modelnew_kernel(tc, x, weight, out):
             max_of_x_units(2, 3)
             max_of_x_units(5, 6)
             clear_signs(6, 7, "scalar")
-            clear_signs(7, 8, "vector")
+            clear_signs(7, 8, "vector", slice(0, K // 2))
+            clear_signs(7, 8, "scalar", slice(K // 2, K))
             max_of_x_units(4, 5)
             max_of_x_units(7, 8)
             clear_signs(8, 10, "scalar")
@@ -202,11 +203,12 @@ def tile_modelnew_kernel(tc, x, weight, out):
             clear_signs(18, 20, "vector")
             clear_signs(20, 22, "vector")
             max_of_w_units(16, 20)
+            clear_signs(22, 23, "scalar")
             for i in range(ROW_TILES):
                 scale_x(1, i)
                 if i == 0:
                     transpose_x(1, 7)
-            clear_signs(22, 24, "vector")
+            clear_signs(23, 24, "vector")
             max_of_w_units(20, 24)
             w_everywhere = spread(w_part_max[:, W_MAXIMA - 1:W_MAXIMA], "w_everywhere")
             warm_up = psum1.tile([P, CHUNK], F32, name="warm_up", tag="bank")
@@ -278,16 +280,30 @@ def tile_modelnew_kernel(tc, x, weight, out):
             nc.vector.tensor_tensor(out=out_factor[:], in0=x_max_over_448[:], in1=w_max_over_448[:],
                                     op=ALU.mult)
             for j in range(1, CHUNKS):
-                for g in range(FIRST_ON_SCALAR, PASSES):
-                    scale_w(j, g, "scalar")
-                for g in range(FIRST_ON_SCALAR):
-                    scale_w(j, g, "vector")
-                    if g > 0:
-                        quantise_w(j, g - 1)
-                for g in range(FIRST_ON_SCALAR - 1, PASSES):
-                    quantise_w(j, g)
-                for i in range(ROW_TILES):
-                    finish(accs[i], i, j - 1, "scalar")
+                if j == 1:
+                    scale_w(1, 2, "scalar")
+                    scale_w(1, 0, "vector")
+                    scale_w(1, 1, "vector")
+                    quantise_w(1, 0)
+                    for i in range(4):
+                        finish(accs[i], i, 0, "scalar")
+                    quantise_w(1, 1)
+                    scale_w(1, 3, "vector")
+                    quantise_w(1, 2)
+                    quantise_w(1, 3)
+                    for i in range(4,ROW_TILES):
+                        finish(accs[i], i, 0, "scalar")
+                else:
+                    for g in range(FIRST_ON_SCALAR, PASSES):
+                        scale_w(j, g, "scalar")
+                    for g in range(FIRST_ON_SCALAR):
+                        scale_w(j, g, "vector")
+                        if g > 0:
+                            quantise_w(j, g - 1)
+                    for g in range(FIRST_ON_SCALAR - 1, PASSES):
+                        quantise_w(j, g)
+                    for i in range(ROW_TILES):
+                        finish(accs[i], i, j - 1, "scalar")
                 in_step = ROW_TILES // 2 if j == 1 else 1
                 for i0 in range(0, ROW_TILES if j < CHUNKS - 1 else ROW_TILES - 1, in_step):
                     for i in range(i0, i0 + in_step):

@@ -33,6 +33,7 @@ FP8_MAX = 448.0
 EPS = 1e-12
 SIGN_BITS_OFF = 0x7FFF7FFF
 TRANSPOSE_BANKS = 7
+SCALE_START = 64
 WARM_UP_MATMULS = 4
 
 FLOPS = 2 * M * K * N
@@ -51,10 +52,12 @@ def tile_modelnew_kernel(tc, x, weight, out):
 
         w_sb = keep.tile([P, W_LOADS, 2 * N], BF16)
         x_sim = keep.tile([P, PASSES, ROW_TILES, PACK * P], BF16, align_bytes=64)
-        x_codes = keep.tile([P, PASSES * ROW_TILES * P], U32, align_bytes=64)
-        x_scale_bytes = keep.tile([P, PASSES * ROW_TILES * P], U8, align_bytes=64)
-        w_codes = keep.tile([P, CHUNKS * PASSES * CHUNK], U32, align_bytes=64)
-        w_scale_bytes = keep.tile([P, CHUNKS * PASSES * CHUNK], U8, align_bytes=64)
+        x_codes = keep.tile([P, PASSES * ROW_TILES * P], U32, align_bytes=256)
+        x_scale_tile = keep.tile([P, SCALE_START + PASSES * ROW_TILES * P], U8, align_bytes=256)
+        x_scale_bytes = x_scale_tile[:, SCALE_START:SCALE_START + PASSES * ROW_TILES * P]
+        w_codes = keep.tile([P, CHUNKS * PASSES * CHUNK], U32, align_bytes=256)
+        w_scale_tile = keep.tile([P, SCALE_START + CHUNKS * PASSES * CHUNK], U8, align_bytes=256)
+        w_scale_bytes = w_scale_tile[:, SCALE_START:SCALE_START + CHUNKS * PASSES * CHUNK]
         identity = keep.tile([P, P], F32)
         identity_bf16 = keep.tile([P, P], BF16)
         spread_out = keep.tile([P, P], F32)
@@ -168,22 +171,21 @@ def tile_modelnew_kernel(tc, x, weight, out):
             clear_signs(0, 1, "vector", slice(0, K // 2))
             clear_signs(0, 1, "vector", slice(K // 2, K))
             max_of_x_units(0, 1)
-            clear_signs(1, 2, "vector")
-            max_of_x_units(1, 2)
-            clear_signs(2, 3, "scalar")
-            clear_signs(3, 4, "vector")
-            max_of_x_units(3, 4)
-            clear_signs(4, 5, "scalar")
-            clear_signs(5, 6, "vector")
+            clear_signs(1, 2, "scalar")
+            clear_signs(2, 3, "vector")
+            clear_signs(3, 4, "scalar")
             max_of_x_units(2, 3)
-            max_of_x_units(5, 6)
-            clear_signs(6, 7, "scalar")
-            clear_signs(7, 8, "vector", slice(0, K // 2))
-            clear_signs(7, 8, "scalar", slice(K // 2, K))
+            max_of_x_units(1, 2)
+            clear_signs(4, 5, "vector")
+            clear_signs(5, 6, "scalar")
+            max_of_x_units(3, 4)
             max_of_x_units(4, 5)
-            max_of_x_units(7, 8)
-            clear_signs(8, 10, "scalar")
+            clear_signs(6, 7, "vector")
+            clear_signs(7, 8, "scalar")
+            max_of_x_units(5, 6)
             max_of_x_units(6, 7)
+            clear_signs(8, 10, "scalar")
+            max_of_x_units(7, 8)
             nc.vector.tensor_reduce(out=x_part_max[:], in_=x_unit_max[:], axis=AX.X, op=ALU.max)
             x_everywhere = spread(x_part_max[:, 0:1], "x_everywhere")
             clear_signs(10, 12, "vector")
@@ -262,6 +264,8 @@ def tile_modelnew_kernel(tc, x, weight, out):
         with tc.psum_pool(name="psum2", bufs=ROW_TILES) as psum2, tc.tile_pool(name="outs", bufs=5) as out_pool:
             scale_w(0, 0, "vector", 0, VECTOR_SHARE)
             scale_w(0, 0, "scalar", VECTOR_SHARE, CHUNK)
+            nc.vector.tensor_tensor(out=out_factor[:], in0=x_max_over_448[:], in1=w_max_over_448[:],
+                                    op=ALU.mult)
             quantise_w(0, 0)
             quantise_x(0, ROW_TILES // 2, ROW_TILES)
             scale_w(0, 1, "scalar")
@@ -277,8 +281,6 @@ def tile_modelnew_kernel(tc, x, weight, out):
             for g in range(PASSES):
                 for i in range(ROW_TILES):
                     mx_pass(accs[i], i, 0, g)
-            nc.vector.tensor_tensor(out=out_factor[:], in0=x_max_over_448[:], in1=w_max_over_448[:],
-                                    op=ALU.mult)
             for j in range(1, CHUNKS):
                 if j == 1:
                     scale_w(1, 2, "scalar")
@@ -314,10 +316,8 @@ def tile_modelnew_kernel(tc, x, weight, out):
                             mx_pass(accs[i], i, j, g)
             for i in range(ROW_TILES - 1):
                 finish(accs[i], i, CHUNKS - 1, "vector" if i % 2 else "scalar")
-            for half in range(2):
-                c0 = half * (CHUNK // 2)
-                half_acc = psum2.tile([P, CHUNK // 2], F32, name="half_acc", tag="acc")
+            for c0, c1, engine in ((0, 256, "vector"), (256, 384, "scalar"), (384, CHUNK, "vector")):
+                last_acc = psum2.tile([P, c1 - c0], F32, name="last_acc", tag="acc")
                 for g in range(PASSES):
-                    mx_pass(half_acc, ROW_TILES - 1, CHUNKS - 1, g, c0, c0 + CHUNK // 2)
-                finish(half_acc, ROW_TILES - 1, CHUNKS - 1, "vector" if half == 0 else "scalar",
-                       c0, c0 + CHUNK // 2)
+                    mx_pass(last_acc, ROW_TILES - 1, CHUNKS - 1, g, c0, c1)
+                finish(last_acc, ROW_TILES - 1, CHUNKS - 1, engine, c0, c1)

@@ -28,7 +28,8 @@ W_MAXIMA = 4
 PAIRS = P
 VECTOR_SHARE = 352
 FIRST_ON_SCALAR = 3
-RUN = 4
+VECTOR_RUN = 4
+SCALAR_RUN = 8
 FP8_MAX = 448.0
 EPS = 1e-12
 SIGN_BITS_OFF = 0x7FFF7FFF
@@ -228,9 +229,10 @@ def tile_modelnew_kernel(tc, x, weight, out):
                 new_panel = slots.tile([P, PACK * CHUNK], BF16, name="panel", tag="slot", align_bytes=64)
                 panels[(j, g)] = new_panel
             panel = panels[(j, g)]
+            run = VECTOR_RUN if engine == "vector" else SCALAR_RUN
             src = w_by_row[:, PACK * g:PACK * g + PACK, j * CHUNK + c0:j * CHUNK + c1].rearrange(
-                "p t (c i) -> p c t i", i=RUN)
-            dst = panel[:, PACK * c0:PACK * c1].rearrange("p (c i t) -> p c t i", i=RUN, t=PACK)
+                "p t (c i) -> p c t i", i=run)
+            dst = panel[:, PACK * c0:PACK * c1].rearrange("p (c i t) -> p c t i", i=run, t=PACK)
             if engine == "vector":
                 nc.vector.tensor_scalar(out=dst, in0=src, scalar1=ws[:, 0:1], scalar2=None,
                                         op0=ALU.mult)

@@ -23,7 +23,7 @@ CHUNKS = N // CHUNK
 W_LOADS = 2 * PASSES
 UNIT = 2048
 UNITS_PER_SCRATCH = 4
-X_MAXIMA = 8
+X_MAXIMA = 10
 W_MAXIMA = 4
 PAIRS = P
 VECTOR_SHARE = 352
@@ -77,7 +77,7 @@ def tile_modelnew_kernel(tc, x, weight, out):
         x_sb = []
         for i in range(ROW_TILES):
             x_tile = slots.tile([P, K], BF16, name="x_tile%d" % i, tag="slot", align_bytes=64)
-            if i == 0:
+            if i < 2:
                 nc.sync.dma_start(out=x_tile[:, 0:K // 2], in_=x_rows[:, i, 0:K // 2])
                 nc.sync.dma_start(out=x_tile[:, K // 2:K], in_=x_rows[:, i, K // 2:K])
             else:
@@ -126,8 +126,8 @@ def tile_modelnew_kernel(tc, x, weight, out):
 
         x_steps = []
 
-        def max_of_x_units(u0, u1):
-            mags = magnitudes(u0, u1)
+        def max_of_x_units(u0, u1, columns=slice(0, K)):
+            mags = magnitudes(u0, u1)[:, columns]
             i = len(x_steps)
             x_steps.append(u0)
             nc.vector.tensor_scalar(out=mags, in0=mags, scalar1=1.0, scalar2=None,
@@ -141,20 +141,33 @@ def tile_modelnew_kernel(tc, x, weight, out):
         with tc.psum_pool(name="psum1", bufs=TRANSPOSE_BANKS) as psum1, tc.tile_pool(name="scratch", bufs=3) as scratch_pool:
             transposed = {}
 
-            def transpose_x(h, i):
-                pairs = x_sb[i][:].bitcast(F32)
+            def transpose_x(g, a):
                 bank = psum1.tile([P, 2, 2, P], F32, name="bank", tag="bank")
-                for gg in range(2):
+                g0 = 2 * PAIRS * g
+                for ii in range(2):
+                    pairs = x_sb[2 * a + ii][:].bitcast(F32)
                     for u in range(2):
-                        g0 = 2 * PAIRS * (2 * h + gg)
-                        nc.tensor.transpose(bank[:, u, gg, :], pairs[:, g0 + u:g0 + 2 * PAIRS:2], identity[:])
-                transposed[(h, i)] = bank
+                        nc.tensor.transpose(bank[:, u, ii, :], pairs[:, g0 + u:g0 + 2 * PAIRS:2], identity[:])
+                transposed[(g, a)] = bank
 
-            def scale_x(h, i):
+            def x_sim_part(g, a):
+                return x_sim[:, g, 2 * a:2 * a + 2, :].rearrange("p i c -> p (i c)")
+
+            def scale_x(g, a):
                 nc.scalar.activation(
-                    out=x_sim[:, 2 * h:2 * h + 2, i, :].rearrange("p g (r u e) -> p g r u e", u=2, e=2),
-                    in_=transposed[(h, i)][:].bitcast(BF16).rearrange("p u g (r e) -> p g r u e", e=2),
+                    out=x_sim_part(g, a).rearrange("p (i r u e) -> p i r u e", i=2, u=2, e=2),
+                    in_=transposed[(g, a)][:].bitcast(BF16).rearrange("p u i (r e) -> p i r u e", e=2),
                     func=ACTF.Copy, scale=xs[:, 0:1])
+
+            def copy_raw_x(g, a):
+                nc.scalar.copy(
+                    out=x_sim_part(g, a).bitcast(F32).rearrange("p (i r u) -> p i r u", i=2, u=2),
+                    in_=transposed[(g, a)][:].rearrange("p u i r -> p i r u"))
+
+            def scale_raw_x(g, a):
+                part = x_sim_part(g, a)
+                nc.gpsimd.tensor_scalar(out=part, in0=part, scalar1=xs[:, 0:1], scalar2=1.0,
+                                        op0=ALU.mult, op1=ALU.mult)
 
             def spread(column, name):
                 everywhere = psum1.tile([P, P], F32, name=name, tag="spread", bufs=1)
@@ -167,16 +180,23 @@ def tile_modelnew_kernel(tc, x, weight, out):
                                         op0=ALU.mult, op1=ALU.max, accum_out=max_over_448[:])
                 nc.vector.reciprocal(out=scale[:], in_=max_over_448[:])
 
-            for i in range(TRANSPOSE_BANKS):
-                transpose_x(0, i)
-            clear_signs(0, 1, "vector", slice(0, K // 2))
-            clear_signs(0, 1, "vector", slice(K // 2, K))
-            max_of_x_units(0, 1)
-            clear_signs(1, 2, "scalar")
+            first_half, second_half = slice(0, K // 2), slice(K // 2, K)
+            parts = [(g, a) for g in range(PASSES) for a in range(ROW_TILES // 2)]
+            for a in range(4):
+                for g in range(2):
+                    if (g, a) != (1, 3):
+                        transpose_x(g, a)
+            clear_signs(0, 1, "vector", first_half)
+            clear_signs(0, 1, "vector", second_half)
+            clear_signs(1, 2, "scalar", first_half)
+            clear_signs(1, 2, "scalar", second_half)
+            max_of_x_units(0, 1, first_half)
+            max_of_x_units(0, 1, second_half)
+            max_of_x_units(1, 2, first_half)
             clear_signs(2, 3, "vector")
+            max_of_x_units(1, 2, second_half)
             clear_signs(3, 4, "scalar")
             max_of_x_units(2, 3)
-            max_of_x_units(1, 2)
             clear_signs(4, 5, "vector")
             clear_signs(5, 6, "scalar")
             max_of_x_units(3, 4)
@@ -191,28 +211,32 @@ def tile_modelnew_kernel(tc, x, weight, out):
             x_everywhere = spread(x_part_max[:, 0:1], "x_everywhere")
             clear_signs(10, 12, "vector")
             scale_from(x_everywhere, x_max_over_448, xs)
-            clear_signs(12, 14, "vector")
             max_of_w_units(8, 12)
-            for i in range(2):
-                scale_x(0, i)
-            transpose_x(0, 7)
-            transpose_x(1, 0)
+            for n in range(3):
+                copy_raw_x(*parts[n])
+                scale_raw_x(*parts[n])
+                transpose_x(*parts[n + 7])
+            clear_signs(12, 14, "vector")
             clear_signs(14, 16, "scalar")
             clear_signs(16, 18, "vector")
+            clear_signs(18, 19, "vector")
+            clear_signs(19, 20, "scalar")
             max_of_w_units(12, 16)
-            for i in range(2, ROW_TILES):
-                scale_x(0, i)
-                transpose_x(1, i - 1)
-            clear_signs(18, 20, "vector")
-            clear_signs(20, 22, "vector")
             max_of_w_units(16, 20)
-            clear_signs(22, 23, "scalar")
-            for i in range(ROW_TILES):
-                scale_x(1, i)
-                if i == 0:
-                    transpose_x(1, 7)
-            clear_signs(23, 24, "vector")
+            for n in range(3, 8):
+                copy_raw_x(*parts[n])
+                scale_raw_x(*parts[n])
+                transpose_x(*parts[n + 7])
+            clear_signs(20, 22, "vector")
+            clear_signs(22, 24, "scalar")
+            scale_x(*parts[8])
+            transpose_x(*parts[15])
             max_of_w_units(20, 24)
+            for n in range(9, 12):
+                copy_raw_x(*parts[n])
+                scale_raw_x(*parts[n])
+            for n in range(12, 16):
+                scale_x(*parts[n])
             w_everywhere = spread(w_part_max[:, W_MAXIMA - 1:W_MAXIMA], "w_everywhere")
             warm_up = psum1.tile([P, CHUNK], F32, name="warm_up", tag="bank")
             for d in range(WARM_UP_MATMULS):

@@ -205,32 +205,40 @@ def tile_modelnew_kernel(tc, x, weight, out):
             clear_signs(7, 8, "scalar")
             max_of_x_units(5, 6)
             max_of_x_units(6, 7)
-            clear_signs(8, 10, "scalar")
+            clear_signs(8, 10, "scalar", slice(K // 2, 2 * K))
             max_of_x_units(7, 8)
+            clear_signs(10, 11, "vector")
             nc.vector.tensor_reduce(out=x_part_max[:], in_=x_unit_max[:], axis=AX.X, op=ALU.max)
             x_everywhere = spread(x_part_max[:, 0:1], "x_everywhere")
-            clear_signs(10, 12, "vector")
+            clear_signs(11, 12, "vector")
+            clear_signs(8, 10, "vector", first_half)
             scale_from(x_everywhere, x_max_over_448, xs)
             max_of_w_units(8, 12)
             for n in range(3):
                 copy_raw_x(*parts[n])
                 scale_raw_x(*parts[n])
                 transpose_x(*parts[n + 7])
+            scale_x(*parts[3])
+            transpose_x(*parts[10])
             clear_signs(12, 14, "vector")
             clear_signs(14, 16, "scalar")
             clear_signs(16, 18, "vector")
-            clear_signs(18, 19, "vector")
-            clear_signs(19, 20, "scalar")
+            clear_signs(18, 19, "vector", slice(0, 3 * K // 4))
+            clear_signs(18, 19, "scalar", slice(3 * K // 4, K))
             max_of_w_units(12, 16)
-            max_of_w_units(16, 20)
-            for n in range(3, 8):
+            for n in range(4, 7):
                 copy_raw_x(*parts[n])
                 scale_raw_x(*parts[n])
                 transpose_x(*parts[n + 7])
+            clear_signs(19, 20, "scalar")
             clear_signs(20, 22, "vector")
-            clear_signs(22, 24, "scalar")
-            scale_x(*parts[8])
-            transpose_x(*parts[15])
+            clear_signs(22, 23, "scalar")
+            max_of_w_units(16, 20)
+            for n in range(7, 9):
+                copy_raw_x(*parts[n])
+                scale_raw_x(*parts[n])
+                transpose_x(*parts[n + 7])
+            clear_signs(23, 24, "scalar")
             max_of_w_units(20, 24)
             for n in range(9, 12):
                 copy_raw_x(*parts[n])

@@ -77,12 +77,12 @@ def tile_modelnew_kernel(tc, x, weight, out):
         x_sb = []
         for i in range(ROW_TILES):
             x_tile = slots.tile([P, K], BF16, name="x_tile%d" % i, tag="slot", align_bytes=64)
-            if i < 2:
-                nc.sync.dma_start(out=x_tile[:, 0:K // 2], in_=x_rows[:, i, 0:K // 2])
-                nc.sync.dma_start(out=x_tile[:, K // 2:K], in_=x_rows[:, i, K // 2:K])
-            else:
-                nc.sync.dma_start(out=x_tile[:], in_=x_rows[:, i, :])
             x_sb.append(x_tile)
+        for columns in (slice(0, K // 2), slice(K // 2, K)):
+            for i in range(2):
+                nc.sync.dma_start(out=x_sb[i][:, columns], in_=x_rows[:, i, columns])
+        for i in range(2, ROW_TILES):
+            nc.sync.dma_start(out=x_sb[i][:], in_=x_rows[:, i, :])
         for c in range(W_LOADS):
             nc.sync.dma_start(out=w_sb[:, c, :], in_=w_rows[:, c // 2, c % 2, :])
 
@@ -187,20 +187,21 @@ def tile_modelnew_kernel(tc, x, weight, out):
                     if (g, a) != (1, 3):
                         transpose_x(g, a)
             clear_signs(0, 1, "vector", first_half)
-            clear_signs(0, 1, "vector", second_half)
             clear_signs(1, 2, "scalar", first_half)
-            clear_signs(1, 2, "scalar", second_half)
             max_of_x_units(0, 1, first_half)
+            clear_signs(0, 1, "vector", second_half)
+            clear_signs(1, 2, "scalar", second_half)
             max_of_x_units(0, 1, second_half)
             max_of_x_units(1, 2, first_half)
-            clear_signs(2, 3, "vector")
+            clear_signs(2, 3, "vector", first_half)
+            clear_signs(2, 3, "scalar", second_half)
             max_of_x_units(1, 2, second_half)
             clear_signs(3, 4, "scalar")
             max_of_x_units(2, 3)
             clear_signs(4, 5, "vector")
             clear_signs(5, 6, "scalar")
-            max_of_x_units(3, 4)
             max_of_x_units(4, 5)
+            max_of_x_units(3, 4)
             clear_signs(6, 7, "vector")
             clear_signs(7, 8, "scalar")
             max_of_x_units(5, 6)
@@ -223,24 +224,19 @@ def tile_modelnew_kernel(tc, x, weight, out):
             clear_signs(12, 14, "vector")
             clear_signs(14, 16, "scalar")
             clear_signs(16, 18, "vector")
-            clear_signs(18, 19, "vector", slice(0, 3 * K // 4))
-            clear_signs(18, 19, "scalar", slice(3 * K // 4, K))
-            max_of_w_units(12, 16)
-            for n in range(4, 7):
-                copy_raw_x(*parts[n])
-                scale_raw_x(*parts[n])
-                transpose_x(*parts[n + 7])
+            clear_signs(18, 19, "vector")
             clear_signs(19, 20, "scalar")
-            clear_signs(20, 22, "vector")
-            clear_signs(22, 23, "scalar")
+            max_of_w_units(12, 16)
             max_of_w_units(16, 20)
-            for n in range(7, 9):
+            for n in range(4, 9):
                 copy_raw_x(*parts[n])
                 scale_raw_x(*parts[n])
                 transpose_x(*parts[n + 7])
-            clear_signs(23, 24, "scalar")
+            clear_signs(20, 22, "vector")
+            clear_signs(22, 24, "scalar")
+            scale_x(*parts[9])
             max_of_w_units(20, 24)
-            for n in range(9, 12):
+            for n in range(10, 12):
                 copy_raw_x(*parts[n])
                 scale_raw_x(*parts[n])
             for n in range(12, 16):

@@ -24,9 +24,9 @@ W_LOADS = 2 * PASSES
 UNIT = 2048
 UNITS_PER_SCRATCH = 4
 X_MAXIMA = 10
-W_MAXIMA = 4
+W_MAXIMA = 5
 PAIRS = P
-VECTOR_SHARE = 352
+VECTOR_SHARE = 384
 FIRST_ON_SCALAR = 3
 VECTOR_RUN = 4
 SCALAR_RUN = 8
@@ -35,7 +35,8 @@ EPS = 1e-12
 SIGN_BITS_OFF = 0x7FFF7FFF
 TRANSPOSE_BANKS = 7
 SCALE_START = 64
-WARM_UP_MATMULS = 4
+EARLY_WARM_UP = 4
+LATE_WARM_UP = 5
 
 FLOPS = 2 * M * K * N
 
@@ -61,7 +62,7 @@ def tile_modelnew_kernel(tc, x, weight, out):
         w_scale_bytes = w_scale_tile[:, SCALE_START:SCALE_START + CHUNKS * PASSES * CHUNK]
         identity = keep.tile([P, P], F32)
         identity_bf16 = keep.tile([P, P], BF16)
-        spread_out = keep.tile([P, P], F32)
+        spread_out = keep.tile([P, 2 * P], F32)
         x_unit_max = keep.tile([P, X_MAXIMA], F32)
         x_part_max = keep.tile([P, 1], F32)
         w_part_max = keep.tile([P, W_MAXIMA], F32)
@@ -120,7 +121,7 @@ def tile_modelnew_kernel(tc, x, weight, out):
             mags = magnitudes(u0, u1)
             n = len(w_steps)
             w_steps.append(u0)
-            first_value = 0.0 if n == 0 else w_part_max[:, n - 1:n]
+            first_value = 0.0 if n < 2 else w_part_max[:, n - 2:n - 1]
             nc.vector.tensor_scalar(out=mags, in0=mags, scalar1=1.0, scalar2=first_value,
                                     op0=ALU.mult, op1=ALU.max, accum_out=w_part_max[:, n:n + 1])
 
@@ -169,15 +170,17 @@ def tile_modelnew_kernel(tc, x, weight, out):
                 nc.gpsimd.tensor_scalar(out=part, in0=part, scalar1=xs[:, 0:1], scalar2=1.0,
                                         op0=ALU.mult, op1=ALU.mult)
 
-            def spread(column, name):
-                everywhere = psum1.tile([P, P], F32, name=name, tag="spread", bufs=1)
-                nc.tensor.matmul(out=everywhere[:], lhsT=column.bitcast(BF16)[:, 1:2].to_broadcast([P, P]),
-                                 rhs=identity_bf16[:], start=True, stop=True)
+            def spread(columns, name):
+                everywhere = psum1.tile([P, len(columns) * P], F32, name=name, tag="spread", bufs=1)
+                for m, column in enumerate(columns):
+                    nc.tensor.matmul(out=everywhere[:, m * P:(m + 1) * P],
+                                     lhsT=column.bitcast(BF16)[:, 1:2].to_broadcast([P, P]),
+                                     rhs=identity_bf16[:], start=True, stop=True)
                 return everywhere
 
-            def scale_from(everywhere, max_over_448, scale):
-                nc.vector.tensor_scalar(out=spread_out[:], in0=everywhere[:], scalar1=1.0 / FP8_MAX, scalar2=EPS / FP8_MAX,
-                                        op0=ALU.mult, op1=ALU.max, accum_out=max_over_448[:])
+            def scale_from(everywhere, width, max_over_448, scale):
+                nc.vector.tensor_scalar(out=spread_out[:, 0:width], in0=everywhere[:], scalar1=1.0 / FP8_MAX,
+                                        scalar2=EPS / FP8_MAX, op0=ALU.mult, op1=ALU.max, accum_out=max_over_448[:])
                 nc.vector.reciprocal(out=scale[:], in_=max_over_448[:])
 
             first_half, second_half = slice(0, K // 2), slice(K // 2, K)
@@ -208,46 +211,52 @@ def tile_modelnew_kernel(tc, x, weight, out):
             max_of_x_units(6, 7)
             clear_signs(8, 10, "scalar", slice(K // 2, 2 * K))
             max_of_x_units(7, 8)
-            clear_signs(10, 11, "vector")
-            nc.vector.tensor_reduce(out=x_part_max[:], in_=x_unit_max[:], axis=AX.X, op=ALU.max)
-            x_everywhere = spread(x_part_max[:, 0:1], "x_everywhere")
-            clear_signs(11, 12, "vector")
             clear_signs(8, 10, "vector", first_half)
-            scale_from(x_everywhere, x_max_over_448, xs)
+            nc.vector.tensor_reduce(out=x_part_max[:], in_=x_unit_max[:], axis=AX.X, op=ALU.max)
+            x_everywhere = spread([x_part_max[:, 0:1]], "x_everywhere")
+            clear_signs(10, 12, "vector")
+            scale_from(x_everywhere, P, x_max_over_448, xs)
             max_of_w_units(8, 12)
             for n in range(3):
                 copy_raw_x(*parts[n])
                 scale_raw_x(*parts[n])
                 transpose_x(*parts[n + 7])
+            clear_signs(12, 14, "scalar")
+            clear_signs(14, 16, "vector")
+            clear_signs(16, 18, "vector")
             scale_x(*parts[3])
             transpose_x(*parts[10])
-            clear_signs(12, 14, "vector")
-            clear_signs(14, 16, "scalar")
-            clear_signs(16, 18, "vector")
-            clear_signs(18, 19, "vector")
-            clear_signs(19, 20, "scalar")
             max_of_w_units(12, 16)
-            max_of_w_units(16, 20)
-            for n in range(4, 9):
+            max_of_w_units(16, 18)
+            for n in range(4, 8):
                 copy_raw_x(*parts[n])
                 scale_raw_x(*parts[n])
                 transpose_x(*parts[n + 7])
+            clear_signs(18, 20, "scalar", slice(3 * K // 4, 2 * K))
+            clear_signs(18, 20, "vector", slice(0, 3 * K // 4))
             clear_signs(20, 22, "vector")
             clear_signs(22, 24, "scalar")
-            scale_x(*parts[9])
-            max_of_w_units(20, 24)
-            for n in range(10, 12):
+            max_of_w_units(18, 20)
+            for n in range(8, 11):
                 copy_raw_x(*parts[n])
                 scale_raw_x(*parts[n])
-            for n in range(12, 16):
-                scale_x(*parts[n])
-            w_everywhere = spread(w_part_max[:, W_MAXIMA - 1:W_MAXIMA], "w_everywhere")
+                if n == 8:
+                    transpose_x(*parts[15])
+            max_of_w_units(20, 24)
             warm_up = psum1.tile([P, CHUNK], F32, name="warm_up", tag="bank")
-            for d in range(WARM_UP_MATMULS):
-                nc.tensor.matmul(out=warm_up[:], lhsT=w_sb[:, 0, 0:P], rhs=w_sb[:, 0, 0:CHUNK],
-                                 start=True, stop=True)
+
+            def warm_up_matmuls(count, values):
+                for d in range(count):
+                    nc.tensor.matmul(out=warm_up[:], lhsT=values[:, 0:P], rhs=values[:, 0:CHUNK], start=True, stop=True)
+
+            for n in range(11, 16):
+                scale_x(*parts[n])
+                if n == 12:
+                    warm_up_matmuls(EARLY_WARM_UP, x_sim_part(*parts[n]))
+            w_everywhere = spread([w_part_max[:, n:n + 1] for n in range(W_MAXIMA - 2, W_MAXIMA)], "w_everywhere")
+            warm_up_matmuls(LATE_WARM_UP, x_sim_part(*parts[12]))
             quantise_x(0, 0, ROW_TILES // 2)
-            scale_from(w_everywhere, w_max_over_448, ws)
+            scale_from(w_everywhere, 2 * P, w_max_over_448, ws)
 
         w_by_row = w_sb[:].rearrange("p c (e n) -> p (c e) n", e=2)
         panels = {}

from contextlib import ExitStack

import concourse.mybir as mybir
from concourse.masks import make_identity

BF16 = mybir.dt.bfloat16
F32 = mybir.dt.float32
I32 = mybir.dt.int32
U32 = mybir.dt.uint32
U8 = mybir.dt.uint8
FP8X4 = mybir.dt.float8_e4m3fn_x4
ALU = mybir.AluOpType
ACTF = mybir.ActivationFunctionType
AX = mybir.AxisListType

P = 128
M, K, N = 1024, 2048, 2048
ROW_TILES = M // P
PACK = 4
PASSES = K // (P * PACK)
CHUNK = 512
CHUNKS = N // CHUNK
W_LOADS = 2 * PASSES
UNIT = 2048
UNITS_PER_SCRATCH = 4
X_MAXIMA = 10
W_MAXIMA = 5
PAIRS = P
VECTOR_SHARE = 384
FIRST_ON_SCALAR = 3
VECTOR_RUN = 4
SCALAR_RUN = 8
FP8_MAX = 448.0
EPS = 1e-12
SIGN_BITS_OFF = 0x7FFF7FFF
TRANSPOSE_BANKS = 7
SCALE_START = 64
EARLY_WARM_UP = 4
LATE_WARM_UP = 5

FLOPS = 2 * M * K * N


def tile_modelnew_kernel(tc, x, weight, out):
    nc = tc.nc
    x_rows = x.flatten_outer_dims().rearrange("(p i) k -> p i k", i=ROW_TILES)
    out_rows = out.flatten_outer_dims().rearrange("(p i) n -> p i n", i=ROW_TILES)
    w_rows = weight.rearrange("(g p u e) n -> p g u (e n)", p=P, u=2, e=2)

    with ExitStack() as ctx:
        keep = ctx.enter_context(tc.tile_pool(name="keep", bufs=1))
        slots = ctx.enter_context(tc.tile_pool(name="slots", bufs=ROW_TILES))
        ctx.enter_context(tc.manual_schedule())

        w_sb = keep.tile([P, W_LOADS, 2 * N], BF16)
        x_sim = keep.tile([P, PASSES, ROW_TILES, PACK * P], BF16, align_bytes=64)
        x_codes = keep.tile([P, PASSES * ROW_TILES * P], U32, align_bytes=256)
        x_scale_tile = keep.tile([P, SCALE_START + PASSES * ROW_TILES * P], U8, align_bytes=256)
        x_scale_bytes = x_scale_tile[:, SCALE_START:SCALE_START + PASSES * ROW_TILES * P]
        w_codes = keep.tile([P, CHUNKS * PASSES * CHUNK], U32, align_bytes=256)
        w_scale_tile = keep.tile([P, SCALE_START + CHUNKS * PASSES * CHUNK], U8, align_bytes=256)
        w_scale_bytes = w_scale_tile[:, SCALE_START:SCALE_START + CHUNKS * PASSES * CHUNK]
        identity = keep.tile([P, P], F32)
        identity_bf16 = keep.tile([P, P], BF16)
        spread_out = keep.tile([P, 2 * P], F32)
        x_unit_max = keep.tile([P, X_MAXIMA], F32)
        x_part_max = keep.tile([P, 1], F32)
        w_part_max = keep.tile([P, W_MAXIMA], F32)
        x_max_over_448 = keep.tile([P, 1], F32)
        w_max_over_448 = keep.tile([P, 1], F32)
        xs = keep.tile([P, 1], F32)
        ws = keep.tile([P, 1], F32)
        out_factor = keep.tile([P, 1], F32)

        make_identity(nc, identity[:])
        nc.vector.tensor_copy(out=identity_bf16[:], in_=identity[:])

        x_sb = []
        for i in range(ROW_TILES):
            x_tile = slots.tile([P, K], BF16, name="x_tile%d" % i, tag="slot", align_bytes=64)
            x_sb.append(x_tile)
        for columns in (slice(0, K // 2), slice(K // 2, K)):
            for i in range(2):
                nc.sync.dma_start(out=x_sb[i][:, columns], in_=x_rows[:, i, columns])
        for i in range(2, ROW_TILES):
            nc.sync.dma_start(out=x_sb[i][:], in_=x_rows[:, i, :])
        for c in range(W_LOADS):
            nc.sync.dma_start(out=w_sb[:, c, :], in_=w_rows[:, c // 2, c % 2, :])

        scratch_tiles = {}

        def raw_units(u0, u1):
            if u0 < ROW_TILES:
                return x_sb[u0][:]
            return w_sb[:].rearrange("p c n -> p (c n)")[:, (u0 - ROW_TILES) * UNIT:(u1 - ROW_TILES) * UNIT]

        def magnitudes(u0, u1):
            t = u0 // UNITS_PER_SCRATCH
            if t not in scratch_tiles:
                new_scratch = scratch_pool.tile([P, UNITS_PER_SCRATCH * UNIT], BF16, name="magnitudes",
                                                tag="magnitudes")
                scratch_tiles[t] = new_scratch
            first = u0 % UNITS_PER_SCRATCH
            return scratch_tiles[t][:, first * UNIT:(first + u1 - u0) * UNIT]

        def clear_signs(u0, u1, engine, columns=None):
            dst = magnitudes(u0, u1)
            src = raw_units(u0, u1)
            if columns is not None:
                dst = dst[:, columns]
                src = src[:, columns]
            if engine == "vector":
                nc.vector.tensor_scalar(out=dst.bitcast(I32), in0=src.bitcast(I32),
                                        scalar1=SIGN_BITS_OFF, scalar2=None, op0=ALU.bitwise_and)
            else:
                nc.scalar.activation(out=dst, in_=src, func=ACTF.Abs)

        w_steps = []

        def max_of_w_units(u0, u1):
            mags = magnitudes(u0, u1)
            n = len(w_steps)
            w_steps.append(u0)
            first_value = 0.0 if n < 2 else w_part_max[:, n - 2:n - 1]
            nc.vector.tensor_scalar(out=mags, in0=mags, scalar1=1.0, scalar2=first_value,
                                    op0=ALU.mult, op1=ALU.max, accum_out=w_part_max[:, n:n + 1])

        x_steps = []

        def max_of_x_units(u0, u1, columns=slice(0, K)):
            mags = magnitudes(u0, u1)[:, columns]
            i = len(x_steps)
            x_steps.append(u0)
            nc.vector.tensor_scalar(out=mags, in0=mags, scalar1=1.0, scalar2=None,
                                    op0=ALU.mult, op1=ALU.max, accum_out=x_unit_max[:, i:i + 1])

        def quantise_x(g, i0, i1):
            a0, a1 = (g * ROW_TILES + i0) * P, (g * ROW_TILES + i1) * P
            nc.vector.quantize_mx(out=x_codes[:, a0:a1].bitcast(FP8X4), scales=x_scale_bytes[:, a0:a1],
                                  in_=x_sim[:, g, i0:i1, :].rearrange("p i c -> p (i c)"))

        with tc.psum_pool(name="psum1", bufs=TRANSPOSE_BANKS) as psum1, tc.tile_pool(name="scratch", bufs=3) as scratch_pool:
            transposed = {}

            def transpose_x(g, a):
                bank = psum1.tile([P, 2, 2, P], F32, name="bank", tag="bank")
                g0 = 2 * PAIRS * g
                for ii in range(2):
                    pairs = x_sb[2 * a + ii][:].bitcast(F32)
                    for u in range(2):
                        nc.tensor.transpose(bank[:, u, ii, :], pairs[:, g0 + u:g0 + 2 * PAIRS:2], identity[:])
                transposed[(g, a)] = bank

            def x_sim_part(g, a):
                return x_sim[:, g, 2 * a:2 * a + 2, :].rearrange("p i c -> p (i c)")

            def scale_x(g, a):
                nc.scalar.activation(
                    out=x_sim_part(g, a).rearrange("p (i r u e) -> p i r u e", i=2, u=2, e=2),
                    in_=transposed[(g, a)][:].bitcast(BF16).rearrange("p u i (r e) -> p i r u e", e=2),
                    func=ACTF.Copy, scale=xs[:, 0:1])

            def copy_raw_x(g, a):
                nc.scalar.copy(
                    out=x_sim_part(g, a).bitcast(F32).rearrange("p (i r u) -> p i r u", i=2, u=2),
                    in_=transposed[(g, a)][:].rearrange("p u i r -> p i r u"))

            def scale_raw_x(g, a):
                part = x_sim_part(g, a)
                nc.gpsimd.tensor_scalar(out=part, in0=part, scalar1=xs[:, 0:1], scalar2=1.0,
                                        op0=ALU.mult, op1=ALU.mult)

            def spread(columns, name):
                everywhere = psum1.tile([P, len(columns) * P], F32, name=name, tag="spread", bufs=1)
                for m, column in enumerate(columns):
                    nc.tensor.matmul(out=everywhere[:, m * P:(m + 1) * P],
                                     lhsT=column.bitcast(BF16)[:, 1:2].to_broadcast([P, P]),
                                     rhs=identity_bf16[:], start=True, stop=True)
                return everywhere

            def scale_from(everywhere, width, max_over_448, scale):
                nc.vector.tensor_scalar(out=spread_out[:, 0:width], in0=everywhere[:], scalar1=1.0 / FP8_MAX,
                                        scalar2=EPS / FP8_MAX, op0=ALU.mult, op1=ALU.max, accum_out=max_over_448[:])
                nc.vector.reciprocal(out=scale[:], in_=max_over_448[:])

            first_half, second_half = slice(0, K // 2), slice(K // 2, K)
            parts = [(g, a) for g in range(PASSES) for a in range(ROW_TILES // 2)]
            for a in range(4):
                for g in range(2):
                    if (g, a) != (1, 3):
                        transpose_x(g, a)
            clear_signs(0, 1, "vector", first_half)
            clear_signs(1, 2, "scalar", first_half)
            max_of_x_units(0, 1, first_half)
            clear_signs(0, 1, "vector", second_half)
            clear_signs(1, 2, "scalar", second_half)
            max_of_x_units(0, 1, second_half)
            max_of_x_units(1, 2, first_half)
            clear_signs(2, 3, "vector", first_half)
            clear_signs(2, 3, "scalar", second_half)
            max_of_x_units(1, 2, second_half)
            clear_signs(3, 4, "scalar")
            max_of_x_units(2, 3)
            clear_signs(4, 5, "vector")
            clear_signs(5, 6, "scalar")
            max_of_x_units(4, 5)
            max_of_x_units(3, 4)
            clear_signs(6, 7, "vector")
            clear_signs(7, 8, "scalar")
            max_of_x_units(5, 6)
            max_of_x_units(6, 7)
            clear_signs(8, 10, "scalar", slice(K // 2, 2 * K))
            max_of_x_units(7, 8)
            clear_signs(8, 10, "vector", first_half)
            nc.vector.tensor_reduce(out=x_part_max[:], in_=x_unit_max[:], axis=AX.X, op=ALU.max)
            x_everywhere = spread([x_part_max[:, 0:1]], "x_everywhere")
            clear_signs(10, 12, "vector")
            scale_from(x_everywhere, P, x_max_over_448, xs)
            max_of_w_units(8, 12)
            for n in range(3):
                copy_raw_x(*parts[n])
                scale_raw_x(*parts[n])
                transpose_x(*parts[n + 7])
            clear_signs(12, 14, "scalar")
            clear_signs(14, 16, "vector")
            clear_signs(16, 18, "vector")
            scale_x(*parts[3])
            transpose_x(*parts[10])
            max_of_w_units(12, 16)
            max_of_w_units(16, 18)
            for n in range(4, 8):
                copy_raw_x(*parts[n])
                scale_raw_x(*parts[n])
                transpose_x(*parts[n + 7])
            clear_signs(18, 20, "scalar", slice(3 * K // 4, 2 * K))
            clear_signs(18, 20, "vector", slice(0, 3 * K // 4))
            clear_signs(20, 22, "vector")
            clear_signs(22, 24, "scalar")
            max_of_w_units(18, 20)
            for n in range(8, 11):
                copy_raw_x(*parts[n])
                scale_raw_x(*parts[n])
                if n == 8:
                    transpose_x(*parts[15])
            max_of_w_units(20, 24)
            warm_up = psum1.tile([P, CHUNK], F32, name="warm_up", tag="bank")

            def warm_up_matmuls(count, values):
                for d in range(count):
                    nc.tensor.matmul(out=warm_up[:], lhsT=values[:, 0:P], rhs=values[:, 0:CHUNK], start=True, stop=True)

            for n in range(11, 16):
                scale_x(*parts[n])
                if n == 12:
                    warm_up_matmuls(EARLY_WARM_UP, x_sim_part(*parts[n]))
            w_everywhere = spread([w_part_max[:, n:n + 1] for n in range(W_MAXIMA - 2, W_MAXIMA)], "w_everywhere")
            warm_up_matmuls(LATE_WARM_UP, x_sim_part(*parts[12]))
            quantise_x(0, 0, ROW_TILES // 2)
            scale_from(w_everywhere, 2 * P, w_max_over_448, ws)

        w_by_row = w_sb[:].rearrange("p c (e n) -> p (c e) n", e=2)
        panels = {}

        def scale_w(j, g, engine, c0=0, c1=CHUNK):
            if c0 == 0:
                new_panel = slots.tile([P, PACK * CHUNK], BF16, name="panel", tag="slot", align_bytes=64)
                panels[(j, g)] = new_panel
            panel = panels[(j, g)]
            run = VECTOR_RUN if engine == "vector" else SCALAR_RUN
            src = w_by_row[:, PACK * g:PACK * g + PACK, j * CHUNK + c0:j * CHUNK + c1].rearrange(
                "p t (c i) -> p c t i", i=run)
            dst = panel[:, PACK * c0:PACK * c1].rearrange("p (c i t) -> p c t i", i=run, t=PACK)
            if engine == "vector":
                nc.vector.tensor_scalar(out=dst, in0=src, scalar1=ws[:, 0:1], scalar2=None,
                                        op0=ALU.mult)
            else:
                nc.scalar.activation(out=dst, in_=src, func=ACTF.Copy, scale=ws[:, 0:1])

        def quantise_w(j, g):
            b = (j * PASSES + g) * CHUNK
            nc.vector.quantize_mx(out=w_codes[:, b:b + CHUNK].bitcast(FP8X4), scales=w_scale_bytes[:, b:b + CHUNK],
                                  in_=panels[(j, g)][:])

        def mx_pass(acc, i, j, g, c0=0, c1=CHUNK):
            a = (g * ROW_TILES + i) * P
            b = (j * PASSES + g) * CHUNK
            nc.tensor.matmul_mx(out=acc[:], lhsT=x_codes[:, a:a + P].bitcast(FP8X4),
                                lhsT_scale=x_scale_bytes[:, a:a + P],
                                rhs=w_codes[:, b + c0:b + c1].bitcast(FP8X4),
                                rhs_scale=w_scale_bytes[:, b + c0:b + c1],
                                start=(g == 0), stop=(g == PASSES - 1))

        def finish(acc, i, j, engine, c0=0, c1=CHUNK):
            result = out_pool.tile([P, CHUNK], F32, name="result", tag="result")
            if engine == "vector":
                nc.vector.tensor_scalar(out=result[:, c0:c1], in0=acc[:], scalar1=out_factor[:, 0:1],
                                        scalar2=None, op0=ALU.mult)
            else:
                nc.scalar.activation(out=result[:, c0:c1], in_=acc[:], func=ACTF.Copy,
                                     scale=out_factor[:, 0:1])
            nc.sync.dma_start(out=out_rows[:, i, j * CHUNK + c0:j * CHUNK + c1], in_=result[:, c0:c1])

        with tc.psum_pool(name="psum2", bufs=ROW_TILES) as psum2, tc.tile_pool(name="outs", bufs=5) as out_pool:
            scale_w(0, 0, "vector", 0, VECTOR_SHARE)
            scale_w(0, 0, "scalar", VECTOR_SHARE, CHUNK)
            nc.vector.tensor_tensor(out=out_factor[:], in0=x_max_over_448[:], in1=w_max_over_448[:],
                                    op=ALU.mult)
            quantise_w(0, 0)
            quantise_x(0, ROW_TILES // 2, ROW_TILES)
            scale_w(0, 1, "scalar")
            scale_w(0, 2, "scalar")
            scale_w(0, 3, "scalar")
            for g in range(1, PASSES):
                quantise_x(g, 0, ROW_TILES)
                quantise_w(0, g)
            accs = {}
            for i in range(ROW_TILES):
                first_acc = psum2.tile([P, CHUNK], F32, name="acc", tag="acc")
                accs[i] = first_acc
            for g in range(PASSES):
                for i in range(ROW_TILES):
                    mx_pass(accs[i], i, 0, g)
            for j in range(1, CHUNKS):
                if j == 1:
                    scale_w(1, 2, "scalar")
                    scale_w(1, 0, "vector")
                    scale_w(1, 1, "vector")
                    quantise_w(1, 0)
                    for i in range(4):
                        finish(accs[i], i, 0, "scalar")
                    quantise_w(1, 1)
                    scale_w(1, 3, "vector")
                    quantise_w(1, 2)
                    quantise_w(1, 3)
                    for i in range(4,ROW_TILES):
                        finish(accs[i], i, 0, "scalar")
                else:
                    for g in range(FIRST_ON_SCALAR, PASSES):
                        scale_w(j, g, "scalar")
                    for g in range(FIRST_ON_SCALAR):
                        scale_w(j, g, "vector")
                        if g > 0:
                            quantise_w(j, g - 1)
                    for g in range(FIRST_ON_SCALAR - 1, PASSES):
                        quantise_w(j, g)
                    for i in range(ROW_TILES):
                        finish(accs[i], i, j - 1, "scalar")
                in_step = ROW_TILES // 2 if j == 1 else 1
                for i0 in range(0, ROW_TILES if j < CHUNKS - 1 else ROW_TILES - 1, in_step):
                    for i in range(i0, i0 + in_step):
                        acc = psum2.tile([P, CHUNK], F32, name="acc", tag="acc")
                        accs[i] = acc
                    for g in range(PASSES):
                        for i in range(i0, i0 + in_step):
                            mx_pass(accs[i], i, j, g)
            for i in range(ROW_TILES - 1):
                finish(accs[i], i, CHUNKS - 1, "vector" if i % 2 else "scalar")
            for c0, c1, engine in ((0, 256, "vector"), (256, 384, "scalar"), (384, CHUNK, "vector")):
                last_acc = psum2.tile([P, c1 - c0], F32, name="last_acc", tag="acc")
                for g in range(PASSES):
                    mx_pass(last_acc, ROW_TILES - 1, CHUNKS - 1, g, c0, c1)
                finish(last_acc, ROW_TILES - 1, CHUNKS - 1, engine, c0, c1)
